import numpy as np
import ml_dtypes


def mxq(x, axis, fmt="e4m3"):
    dtype, down = {"e4m3": (ml_dtypes.float8_e4m3fn, 7), "e5m2": (ml_dtypes.float8_e5m2, 14)}[fmt]
    v = np.moveaxis(np.asarray(x, np.float32).astype(ml_dtypes.bfloat16).astype(np.float64), axis, -1)
    blocks = v.reshape(v.shape[:-1] + (-1, 32))
    amax = np.abs(blocks).max(-1, keepdims=True)
    byte = np.maximum(np.where(amax > 0, np.frexp(amax)[1] - 1 + 127, 0) - down, 1)
    scale = np.exp2(byte - 127.0)
    codes = (blocks / scale).astype(np.float32).astype(dtype).astype(np.float64)
    return np.moveaxis((codes * scale).reshape(v.shape), -1, axis)


WIDE = False


def mx_kscale(k):
    if not WIDE:
        return np.ones(k)
    levels = np.array([10, -10, 5, -5, 0])
    a = np.random.permutation(np.resize(levels, k // 512 * 4)).reshape(k // 512, 4)
    idx = np.arange(k)
    return np.exp2(a[idx // 512, idx % 128 // 32])


BF16 = ml_dtypes.bfloat16


def bf(x):
    return np.asarray(x, np.float32).astype(BF16)


def f64(x):
    return np.asarray(x).astype(np.float64)


B, C, H, W, HID, D, K = 8, 1536, 32, 32, 512, 128, 64
N = H * W
ITERS = 3


def lse(a, axis):
    m = a.max(axis=axis, keepdims=True)
    return np.squeeze(m, axis=axis) + np.log(np.exp(a - m).sum(axis=axis))


def sinkhorn_log(S, num_iters=ITERS):
    b, m, n = S.shape
    norm = -np.log(float(n))
    log_a = np.full((b, m), norm)
    log_b = np.full((b, n), norm)
    u = np.zeros((b, m))
    v = np.zeros((b, n))
    for _ in range(num_iters):
        u = log_a - lse(S + v[:, None, :], 2)
        v = log_b - lse(S + u[:, :, None], 1)
    return S + u[:, :, None] + v[:, None, :] - norm


def setup_inputs():
    t = mx_kscale(HID)
    return {
        "h_cluster": bf(np.maximum(np.random.standard_normal((B, HID, N)), 0.0) * t[None, :, None]),
        "w2c": bf(np.random.standard_normal((D, HID)) / np.sqrt(HID) / t[None, :]),
        "b2c": bf(np.random.standard_normal(D) * 0.1),
        "scores": bf(np.random.standard_normal((B, K, N)) * 2.0),
        "temperature": bf(np.atleast_1d(1.5 + 0.1 * np.random.standard_normal())),
    }


def reference(h_cluster, w2c, b2c, scores, temperature):
    f = (mxq(f64(w2c), 1, "e4m3") @ mxq(f64(h_cluster), 1, "e4m3")) + f64(b2c)[None, :, None]
    log_p = sinkhorn_log(f64(scores))
    p = np.exp(log_p / f64(temperature)) + np.exp(log_p)
    agg = mxq(f, 2, "e4m3") @ mxq(p, 2, "e4m3").transpose(0, 2, 1)
    flat = agg.reshape(agg.shape[0], -1)
    nrm = np.maximum(np.sqrt((flat ** 2).sum(-1, keepdims=True)), 1e-12)
    return flat / nrm

@@ -1,0 +1,532 @@
+from contextlib import ExitStack
+
+import concourse.mybir as mybir
+from concourse.masks import make_identity
+
+F32 = mybir.dt.float32
+BF16 = mybir.dt.bfloat16
+U32 = mybir.dt.uint32
+U8 = mybir.dt.uint8
+FP8X4 = mybir.dt.float8_e4m3fn_x4
+ALU = mybir.AluOpType
+ACT = mybir.ActivationFunctionType
+AX = mybir.AxisListType
+
+P = 128
+B, HID, N, D, K = 8, 512, 1024, 128, 64
+Q = B // 2
+NT = N // P
+HALF = N // 2
+
+FLOPS = 2 * B * (D * HID * N + D * K * N)
+
+REGROUP = ("s", "g", "s", "s")
+PLAN = {}
+ADD_ENGINE = "g"
+
+
+def tile_image_aggregation_pa_kernel(tc, h_cluster, w2c, b2c, scores, temperature, out):
+    nc = tc.nc
+    with ExitStack() as ctx:
+        const = ctx.enter_context(tc.tile_pool(name="const", bufs=1))
+        keep = ctx.enter_context(tc.tile_pool(name="keep", bufs=1))
+        work = ctx.enter_context(tc.tile_pool(name="work", bufs=3))
+        small = ctx.enter_context(tc.tile_pool(name="small", bufs=2))
+        hraw = ctx.enter_context(tc.tile_pool(name="hraw", bufs=6))
+        hwork = ctx.enter_context(tc.tile_pool(name="hwork", bufs=3))
+        ps_tr = ctx.enter_context(tc.psum_pool(name="ps_tr", bufs=3))
+        ps_f = ctx.enter_context(tc.psum_pool(name="ps_f", bufs=2))
+        ps_mv = ctx.enter_context(tc.psum_pool(name="ps_mv", bufs=2))
+        ps_misc = ctx.enter_context(tc.psum_pool(name="ps_misc", bufs=1))
+
+        s_a = keep.tile([P, Q, N], BF16)
+        s_view = scores.rearrange("(q i) k n -> (i k) q n", i=2)
+        for q in range(Q):
+            nc.sync.dma_start(out=s_a[:, q, :], in_=s_view[:, q, :])
+        bias_bc = const.tile([P, D], BF16)
+        nc.scalar.dma_start(out=bias_bc[:], in_=b2c.partition_broadcast(P))
+        temp = const.tile([P, 1], BF16)
+        nc.scalar.dma_start(out=temp[:], in_=temperature.partition_broadcast(P))
+        w_sb = const.tile([P, HID], BF16)
+        nc.sync.dma_start(out=w_sb[:], in_=w2c)
+        raws = []
+        for b in range(B):
+            raw = hraw.tile([P, 4, N], BF16, tag="raw")
+            nc.sync.dma_start(out=raw[:], in_=h_cluster[b].rearrange("(p j) n -> p j n", j=4))
+            raws.append(raw)
+
+        ident_f = const.tile([P, P], F32)
+        make_identity(nc, ident_f[:])
+        ident_b = const.tile([P, P], BF16)
+        make_identity(nc, ident_b[:])
+        ones_f = const.tile([P, P], F32)
+        nc.vector.memset(ones_f[:], 1.0)
+        mask = const.tile([P, 2, 2], F32)
+        nc.vector.memset(mask[:], 0.0)
+        nc.vector.memset(mask[0:64, :, 0:1], 1.0)
+        nc.vector.memset(mask[64:128, :, 1:2], 1.0)
+
+        m_row = keep.tile([P, Q], F32)
+        r1 = keep.tile([P, Q], F32)
+        d_a = keep.tile([P, Q, N], F32)
+        mn = keep.tile([P, Q * NT, 2], F32)
+        hl_b = keep.tile([P, Q, 2, NT, P], BF16)
+        hl_a = keep.tile([P, Q, 2, N], BF16)
+        pc = keep.tile([P, Q, 2 * P], U32, align_bytes=64)
+        psc = keep.tile([P, Q, 2 * P], U8, align_bytes=64)
+        fc = keep.tile([P, B, 2 * D], U32, align_bytes=64)
+        fs = keep.tile([P, B, 2 * D], U8, align_bytes=64)
+        wc = const.tile([P, D], U32, align_bytes=64)
+        ws = const.tile([P, D], U8, align_bytes=64)
+        inv_t = const.tile([P, 1], F32)
+        agg = keep.tile([P, B, K], F32)
+        ss = keep.tile([P, B], F32)
+
+        def w_path_1():
+            w_perm = const.tile([P, 4, P], BF16)
+            nc.vector.tensor_copy(out=w_perm[:], in_=w_sb[:].rearrange("d (p j) -> d j p", j=4))
+            wps = ps_misc.tile([P, 4, D], BF16, tag="misc")
+            for j in range(4):
+                nc.tensor.transpose(wps[:, j, :], w_perm[:, j, :], ident_b[:])
+            return wps
+
+        def w_path_2(wps):
+            wg = const.tile([P, D, 4], BF16, align_bytes=64)
+            nc.vector.tensor_copy(out=wg[:], in_=wps[:].rearrange("p j d -> p d j"))
+            nc.vector.reciprocal(out=inv_t[:], in_=temp[:])
+            nc.vector.quantize_mx(out=wc[:].bitcast(FP8X4), scales=ws[:], in_=wg[:].rearrange("p d j -> p (d j)"))
+
+        state = {"r": 0, "q": 0, "f": 0}
+        grps, hcs, fbs, fgs = {}, {}, {}, {}
+
+        def fill_r(count):
+            for x in range(count):
+                u = state["r"]
+                if u >= 2 * B:
+                    return
+                state["r"] = u + 1
+                b, g = divmod(u, 2)
+                if g == 0:
+                    grps[b] = hwork.tile([P, N, 4], BF16, tag="grp", name="grp", align_bytes=64)
+                for c in (2 * g, 2 * g + 1):
+                    dst = grps[b][:, c * 256 : (c + 1) * 256, :].rearrange("p (c i) t -> p c t i", i=4)
+                    src = raws[b][:, :, c * 256 : (c + 1) * 256].rearrange("p t (c i) -> p c t i", i=4)
+                    eng = REGROUP[(4 * b + c) % len(REGROUP)]
+                    if eng == "v":
+                        nc.vector.tensor_copy(out=dst, in_=src)
+                    elif eng == "s":
+                        nc.scalar.copy(out=dst, in_=src)
+                    else:
+                        nc.gpsimd.tensor_scalar(out=dst, in0=src, scalar1=1.0, scalar2=0.0, op0=ALU.mult, op1=ALU.add)
+
+        def fill_q(count):
+            for x in range(count):
+                u = state["q"]
+                if u >= 2 * B or u >= state["r"]:
+                    return
+                state["q"] = u + 1
+                b, g = divmod(u, 2)
+                if g == 0:
+                    hcs[b] = (
+                        hwork.tile([P, N], U32, tag="hc", name="hc", align_bytes=64),
+                        hwork.tile([P, N], U8, tag="hs", name="hs", align_bytes=64),
+                    )
+                hc, hs = hcs[b]
+                nc.vector.quantize_mx(
+                    out=hc[:, g * HALF : (g + 1) * HALF].bitcast(FP8X4),
+                    scales=hs[:, g * HALF : (g + 1) * HALF],
+                    in_=grps[b][:, g * HALF : (g + 1) * HALF, :].rearrange("p n j -> p (n j)"),
+                )
+                fb = ps_f.tile([P, 4, D], F32, tag="f", name="fb")
+                fbs[u] = fb
+                for j in range(4):
+                    nt = 4 * g + j
+                    nc.tensor.matmul_mx(
+                        out=fb[:, j, :],
+                        lhsT=hc[:, nt * P : (nt + 1) * P].bitcast(FP8X4),
+                        lhsT_scale=hs[:, nt * P : (nt + 1) * P],
+                        rhs=wc[:].bitcast(FP8X4),
+                        rhs_scale=ws[:],
+                        start=True,
+                        stop=True,
+                    )
+
+        def fill_f(count):
+            for x in range(count):
+                u = state["f"]
+                if u >= 2 * B or u >= state["q"]:
+                    return
+                state["f"] = u + 1
+                b, g = divmod(u, 2)
+                fg = hwork.tile([P, D, 4], BF16, tag="fg", name="fg", align_bytes=64)
+                nc.vector.tensor_tensor(
+                    out=fg[:],
+                    in0=fbs[u][:].rearrange("p j d -> p d j"),
+                    in1=bias_bc[:].unsqueeze(2).to_broadcast([P, D, 4]),
+                    op=ALU.add,
+                )
+                fgs[u] = fg
+                if u >= 1:
+                    quant_f(u - 1)
+
+        def quant_f(u):
+            b, g = divmod(u, 2)
+            nc.vector.quantize_mx(
+                out=fc[:, b, g * D : (g + 1) * D].bitcast(FP8X4),
+                scales=fs[:, b, g * D : (g + 1) * D],
+                in_=fgs[u][:].rearrange("p d j -> p (d j)"),
+            )
+
+        def fill(key):
+            r, qq, f = PLAN.get(key, (0, 0, 0))
+            fill_f(f)
+            fill_q(qq)
+            fill_r(r)
+
+        def rowmax(q):
+            nc.vector.tensor_reduce(out=m_row[:, q : q + 1], in_=s_a[:, q, :], axis=AX.X, op=ALU.max)
+
+        def junk(q):
+            jk = work.tile([P, N], BF16, tag="jk")
+            nm = small.tile([P, 1], F32, tag="nm")
+            nc.scalar.mul(out=nm[:], in_=m_row[:, q : q + 1], mul=-1.0)
+            nc.scalar.activation(
+                out=jk[:], in_=s_a[:, q, :], func=ACT.Exp, bias=nm[:, 0:1], accum_out=r1[:, q : q + 1]
+            )
+
+        def d_half(hh):
+            q, h = divmod(hh, 2)
+            sl = slice(h * HALF, (h + 1) * HALF)
+            nc.gpsimd.tensor_scalar(
+                out=d_a[:, q, sl], in0=s_a[:, q, sl], scalar1=-1.0, scalar2=m_row[:, q : q + 1],
+                op0=ALU.mult, op1=ALU.add,
+            )
+
+        dpss, z1s, ebs, tpss = {}, {}, {}, {}
+
+        def tr_d(hh):
+            q, h = divmod(hh, 2)
+            dps = ps_tr.tile([P, 4, P], F32, tag="tr", name="dps")
+            for t in range(4):
+                nt = 4 * h + t
+                nc.tensor.transpose(dps[:, t, :], d_a[:, q, nt * P : (nt + 1) * P], ident_f[:])
+            dpss[hh] = dps
+
+        def min_z(hh):
+            dview = dpss[hh][:].rearrange("p t (i k) -> p (t i) k", i=2)
+            mslice = mn[:, 4 * hh : 4 * hh + 4, :].rearrange("p t i -> p (t i)")
+            nc.vector.tensor_reduce(out=mslice, in_=dview, axis=AX.X, op=ALU.min)
+            z1 = work.tile([P, 8, K], F32, tag="z1")
+            nc.vector.tensor_tensor(
+                out=z1[:], in0=mslice.unsqueeze(2).to_broadcast([P, 8, K]), in1=dview, op=ALU.subtract
+            )
+            z1s[hh] = z1
+
+        def exp_e(hh):
+            e_b = work.tile([P, HALF], F32, tag="e_b")
+            nc.scalar.activation(out=e_b[:], in_=z1s[hh][:].rearrange("p g k -> p (g k)"), func=ACT.Exp)
+            ebs[hh] = e_b
+
+        def hi_e(hh):
+            q, h = divmod(hh, 2)
+            nc.vector.tensor_copy(
+                out=hl_b[:, q, 0, 4 * h : 4 * h + 4, :].rearrange("p t c -> p (t c)"), in_=ebs[hh][:]
+            )
+
+        def lo_e(hh):
+            q, h = divmod(hh, 2)
+            nc.gpsimd.tensor_tensor(
+                out=hl_b[:, q, 1, 4 * h : 4 * h + 4, :].rearrange("p t c -> p (t c)"),
+                in0=ebs[hh][:],
+                in1=hl_b[:, q, 0, 4 * h : 4 * h + 4, :].rearrange("p t c -> p (t c)"),
+                op=ALU.subtract,
+            )
+
+        def tr_e(hh):
+            q, h = divmod(hh, 2)
+            tps = ps_tr.tile([P, 2, 4, P], BF16, tag="tr", name="tps")
+            for s in range(2):
+                for t in range(4):
+                    nc.tensor.transpose(tps[:, s, t, :], hl_b[:, q, s, 4 * h + t, :], ident_b[:])
+            tpss[hh] = tps
+
+        def evac_e(hh):
+            q, h = divmod(hh, 2)
+            nc.scalar.copy(
+                out=hl_a[:, q, :, h * HALF : (h + 1) * HALF], in_=tpss[hh][:].rearrange("p s t n -> p s (t n)")
+            )
+
+        def split(dst, src):
+            nc.vector.tensor_copy(out=dst[:, :, 0, :], in_=src)
+            nc.vector.tensor_tensor(out=dst[:, :, 1, :], in0=src, in1=dst[:, :, 0, :], op=ALU.subtract)
+
+        chain = {}
+
+        def alpha_from(bt, rsum):
+            ra = small.tile([P, 2, 2], F32, tag="ra%d" % bt)
+            nc.vector.reciprocal(out=ra[:], in_=rsum)
+            am32 = small.tile([P, 2, 2], F32, tag="am32%d" % bt)
+            nc.vector.tensor_tensor(out=am32[:], in0=ra[:], in1=mask[:], op=ALU.mult)
+            am = small.tile([P, 2, 2, 2], BF16, tag="am%d" % bt)
+            split(am, am32[:])
+            chain[bt] = {"am": am, "am32": am32}
+
+        def u_mm(bt):
+            rps = ps_mv.tile([P, 2, 2, 2], F32, tag="mv", name="rps")
+            beta = chain[bt]["bt"]
+            for ql in range(2):
+                q = 2 * bt + ql
+                step = 0
+                for nt in range(NT):
+                    for s in range(2):
+                        nc.tensor.matmul(
+                            out=rps[:, ql].rearrange("p s i -> p (s i)"),
+                            lhsT=hl_b[:, q, s, nt, :],
+                            rhs=beta[:, ql * NT + nt].rearrange("p s i -> p (s i)"),
+                            start=(step == 0),
+                            stop=(step == 2 * NT - 1),
+                        )
+                        step += 1
+            chain[bt]["rps"] = rps
+
+        def u_hop(bt):
+            rs = small.tile([P, 2, 2], F32, tag="rs%d" % bt)
+            nc.vector.tensor_reduce(
+                out=rs[:], in_=chain[bt]["rps"][:].rearrange("p q s i -> p q i s"), axis=AX.X, op=ALU.add
+            )
+            alpha_from(bt, rs[:])
+
+        def v_mm(bt):
+            cps = ps_mv.tile([P, 2 * NT, 2, 2], F32, tag="mv", name="cps")
+            am = chain[bt]["am"]
+            for ql in range(2):
+                q = 2 * bt + ql
+                for nt in range(NT):
+                    for s in range(2):
+                        nc.tensor.matmul(
+                            out=cps[:, ql * NT + nt].rearrange("p s i -> p (s i)"),
+                            lhsT=hl_a[:, q, s, nt * P : (nt + 1) * P],
+                            rhs=am[:, ql].rearrange("p s i -> p (s i)"),
+                            start=(s == 0),
+                            stop=(s == 1),
+                        )
+            chain[bt]["cps"] = cps
+
+        def v_hop(bt, last):
+            cs = small.tile([P, 2 * NT, 2], F32, tag="cs%d" % bt)
+            nc.vector.tensor_reduce(
+                out=cs[:], in_=chain[bt]["cps"][:].rearrange("p g s i -> p g i s"), axis=AX.X, op=ALU.add
+            )
+            chain[bt]["cs"] = cs
+            if not last:
+                b32 = small.tile([P, 2 * NT, 2], F32, tag="b32%d" % bt)
+                nc.vector.reciprocal(out=b32[:], in_=cs[:])
+                beta = small.tile([P, 2 * NT, 2, 2], BF16, tag="bt%d" % bt)
+                split(beta, b32[:])
+                chain[bt]["bt"] = beta
+
+        def ln_alpha(bt):
+            a_sel = small.tile([P, 2], F32, tag="a_sel%d" % bt)
+            nc.vector.tensor_reduce(out=a_sel[:], in_=chain[bt]["am32"][:], axis=AX.X, op=ALU.add)
+            ln_a = small.tile([P, 2], F32, tag="ln_a%d" % bt)
+            nc.scalar.activation(out=ln_a[:], in_=a_sel[:], func=ACT.Ln)
+            chain[bt]["ln_a"] = ln_a
+
+        yas, ypss, zfs, q12, pgs = {}, {}, {}, {}, {}
+
+        def y_half(hh):
+            q, h = divmod(hh, 2)
+            y_a = work.tile([P, HALF], F32, tag="y_a")
+            nc.gpsimd.tensor_scalar(
+                out=y_a[:], in0=d_a[:, q, h * HALF : (h + 1) * HALF], scalar1=-1.0,
+                scalar2=chain[q // 2]["ln_a"][:, q % 2 : q % 2 + 1], op0=ALU.mult, op1=ALU.add,
+            )
+            yas[hh] = y_a
+
+        def tr_y(hh):
+            yps = ps_tr.tile([P, 4, P], F32, tag="tr", name="yps")
+            for t in range(4):
+                nc.tensor.transpose(yps[:, t, :], yas[hh][:, t * P : (t + 1) * P], ident_f[:])
+            ypss[hh] = yps
+
+        def ln_c(bt):
+            lc = small.tile([P, 2 * NT, 2], F32, tag="lc%d" % bt)
+            nc.scalar.activation(out=lc[:], in_=chain[bt]["cs"][:], func=ACT.Ln)
+            bias_f = small.tile([P, 2 * NT, 2], F32, tag="bias_f%d" % bt)
+            nc.vector.tensor_tensor(
+                out=bias_f[:], in0=mn[:, bt * 2 * NT : (bt + 1) * 2 * NT, :], in1=lc[:], op=ALU.subtract
+            )
+            chain[bt]["bias_f"] = bias_f
+
+        def z_f(hh):
+            bt, loc = divmod(hh, 4)
+            zf = work.tile([P, 8, K], F32, tag="zf")
+            bslice = chain[bt]["bias_f"][:, 4 * loc : 4 * loc + 4, :].rearrange("p t i -> p (t i)")
+            nc.vector.tensor_tensor(
+                out=zf[:],
+                in0=bslice.unsqueeze(2).to_broadcast([P, 8, K]),
+                in1=ypss[hh][:].rearrange("p t (i k) -> p (t i) k", i=2),
+                op=ALU.add,
+            )
+            zfs[hh] = zf
+
+        def exps(hh):
+            zflat = zfs[hh][:].rearrange("p g k -> p (g k)")
+            q1 = work.tile([P, HALF], F32, tag="q1")
+            nc.scalar.activation(out=q1[:], in_=zflat, func=ACT.Exp)
+            q2 = work.tile([P, HALF], F32, tag="q2")
+            nc.scalar.activation(out=q2[:], in_=zflat, func=ACT.Exp, scale=inv_t[:, 0:1])
+            q12[hh] = (q1, q2)
+
+        def add_p(hh):
+            q1, q2 = q12[hh]
+            pg = work.tile([P, P, 4], BF16, tag="pg", align_bytes=64)
+            eng = nc.gpsimd if ADD_ENGINE == "g" else nc.vector
+            eng.tensor_tensor(
+                out=pg[:],
+                in0=q1[:].rearrange("p (j c) -> p c j", j=4),
+                in1=q2[:].rearrange("p (j c) -> p c j", j=4),
+                op=ALU.add,
+            )
+            pgs[hh] = pg
+
+        def quant_p(hh):
+            q, g = divmod(hh, 2)
+            nc.vector.quantize_mx(
+                out=pc[:, q, g * P : (g + 1) * P].bitcast(FP8X4),
+                scales=psc[:, q, g * P : (g + 1) * P],
+                in_=pgs[hh][:].rearrange("p c j -> p (c j)"),
+            )
+
+        def agg_mm(b):
+            q, i = divmod(b, 2)
+            aps = ps_misc.tile([P, 2 * K], F32, tag="misc", name="aps")
+            for g in range(2):
+                nc.tensor.matmul_mx(
+                    out=aps[:],
+                    lhsT=fc[:, b, g * D : (g + 1) * D].bitcast(FP8X4),
+                    lhsT_scale=fs[:, b, g * D : (g + 1) * D],
+                    rhs=pc[:, q, g * P : (g + 1) * P].bitcast(FP8X4),
+                    rhs_scale=psc[:, q, g * P : (g + 1) * P],
+                    start=(g == 0),
+                    stop=(g == 1),
+                )
+            nc.scalar.copy(out=agg[:, b, :], in_=aps[:, i * K : (i + 1) * K])
+            sq = small.tile([P, K], F32, tag="sq")
+            nc.scalar.activation(out=sq[:], in_=agg[:, b, :], func=ACT.Square, accum_out=ss[:, b : b + 1])
+
+        rowmax(0)
+        junk(0)
+        d_half(0)
+        d_half(1)
+        rowmax(1)
+        junk(1)
+        tr_d(0)
+        wps = w_path_1()
+        steps0 = ["v", "u", "v", "u", "v"]
+        done = {0: 0, 1: 0}
+
+        def chain_mm(bt):
+            kind = steps0[done[bt]]
+            if kind == "v":
+                v_mm(bt)
+            else:
+                u_mm(bt)
+
+        def chain_hop(bt):
+            kind = steps0[done[bt]]
+            last = done[bt] == 4
+            if kind == "v":
+                v_hop(bt, last)
+            else:
+                u_hop(bt)
+                if done[bt] == 3:
+                    ln_alpha(bt)
+            done[bt] += 1
+
+        for tick in range(11):
+            if tick < 8:
+                min_z(tick)
+                exp_e(tick)
+            if tick + 2 < 8:
+                d_half(tick + 2)
+            if tick + 1 < 8:
+                tr_d(tick + 1)
+            if tick in (1, 3):
+                rowmax(tick // 2 + 2)
+                junk(tick // 2 + 2)
+            if 1 <= tick < 9:
+                hi_e(tick - 1)
+                lo_e(tick - 1)
+                tr_e(tick - 1)
+            if tick == 2:
+                w_path_2(wps)
+            if 2 <= tick < 10:
+                evac_e(tick - 2)
+            if tick == 5:
+                alpha_from(0, r1[:, 0:2].unsqueeze(2).to_broadcast([P, 2, 2]))
+            if tick == 6:
+                chain_mm(0)
+            if tick >= 7:
+                chain_hop(0)
+                chain_mm(0)
+            if tick == 9:
+                alpha_from(1, r1[:, 2:4].unsqueeze(2).to_broadcast([P, 2, 2]))
+            if tick == 10:
+                chain_mm(1)
+            fill("a%d" % tick)
+
+        for hh in range(4):
+            y_half(hh)
+        chain_hop(0)
+        ln_c(0)
+        fill("b0")
+        for r in range(4):
+            chain_hop(1)
+            chain_mm(1)
+            fill("c%d" % r)
+            tr_y(r)
+            z_f(r)
+            exps(r)
+            fill("d%d" % r)
+            add_p(r)
+            fill("e%d" % r)
+            quant_p(r)
+            if r % 2 == 1:
+                fill("f%d" % r)
+        for hh in range(4, 8):
+            y_half(hh)
+        fill("g")
+        chain_hop(1)
+        ln_c(1)
+        for r in range(4, 8):
+            tr_y(r)
+            z_f(r)
+            exps(r)
+            fill("h%d" % r)
+            if r > 4:
+                add_p(r - 1)
+                quant_p(r - 1)
+        fill_r(99)
+        fill_q(99)
+        fill_f(99)
+        fill_q(99)
+        fill_f(99)
+        quant_f(2 * B - 1)
+        add_p(7)
+        quant_p(7)
+        for b in range(B):
+            agg_mm(b)
+        tot = ps_mv.tile([P, B], F32, tag="mv")
+        nc.tensor.matmul(out=tot[:], lhsT=ones_f[:], rhs=ss[:], start=True, stop=True)
+        tmax = small.tile([P, B], F32, tag="tmax")
+        nc.vector.tensor_scalar_max(out=tmax[:], in0=tot[:], scalar1=1e-24)
+        nrm = small.tile([P, B], F32, tag="nrm")
+        nc.scalar.activation(out=nrm[:], in_=tmax[:], func=ACT.Sqrt)
+        rn = small.tile([P, B], F32, tag="rn")
+        nc.vector.reciprocal(out=rn[:], in_=nrm[:])
+        res = keep.tile([P, B, K], F32)
+        nc.vector.tensor_tensor(
+            out=res[:], in0=agg[:], in1=rn[:].unsqueeze(2).to_broadcast([P, B, K]), op=ALU.mult
+        )
+        nc.sync.dma_start(out=out.rearrange("b (d k) -> d b k", k=K), in_=res[:])

@@ -20,9 +20,10 @@ HALF = N // 2
 
 FLOPS = 2 * B * (D * HID * N + D * K * N)
 
-REGROUP = ("s", "g", "s", "s")
+REGROUP = ("v", "s", "v", "v", "s", "v", "s", "v")
 PLAN = {}
-ADD_ENGINE = "g"
+ADD_ENGINE = "v"
+OPT = {"d": "s", "y": "s", "z1": "s", "lo": "g"}
 
 
 def tile_image_aggregation_pa_kernel(tc, h_cluster, w2c, b2c, scores, temperature, out):
@@ -194,13 +195,18 @@ def tile_image_aggregation_pa_kernel(tc, h_cluster, w2c, b2c, scores, temperatur
                 out=jk[:], in_=s_a[:, q, :], func=ACT.Exp, bias=nm[:, 0:1], accum_out=r1[:, q : q + 1]
             )
 
+        def affine(eng, dst, src, col):
+            if eng == "s":
+                nc.scalar.activation(out=dst, in_=src, func=ACT.Identity, bias=col, scale=-1.0)
+            elif eng == "v":
+                nc.vector.tensor_scalar(out=dst, in0=src, scalar1=-1.0, scalar2=col, op0=ALU.mult, op1=ALU.add)
+            else:
+                nc.gpsimd.tensor_scalar(out=dst, in0=src, scalar1=-1.0, scalar2=col, op0=ALU.mult, op1=ALU.add)
+
         def d_half(hh):
             q, h = divmod(hh, 2)
             sl = slice(h * HALF, (h + 1) * HALF)
-            nc.gpsimd.tensor_scalar(
-                out=d_a[:, q, sl], in0=s_a[:, q, sl], scalar1=-1.0, scalar2=m_row[:, q : q + 1],
-                op0=ALU.mult, op1=ALU.add,
-            )
+            affine(OPT["d"], d_a[:, q, sl], s_a[:, q, sl], m_row[:, q : q + 1])
 
         dpss, z1s, ebs, tpss = {}, {}, {}, {}
 
@@ -216,15 +222,25 @@ def tile_image_aggregation_pa_kernel(tc, h_cluster, w2c, b2c, scores, temperatur
             dview = dpss[hh][:].rearrange("p t (i k) -> p (t i) k", i=2)
             mslice = mn[:, 4 * hh : 4 * hh + 4, :].rearrange("p t i -> p (t i)")
             nc.vector.tensor_reduce(out=mslice, in_=dview, axis=AX.X, op=ALU.min)
-            z1 = work.tile([P, 8, K], F32, tag="z1")
-            nc.vector.tensor_tensor(
-                out=z1[:], in0=mslice.unsqueeze(2).to_broadcast([P, 8, K]), in1=dview, op=ALU.subtract
-            )
-            z1s[hh] = z1
+            if OPT["z1"] == "v":
+                z1 = work.tile([P, 8, K], F32, tag="z1")
+                nc.vector.tensor_tensor(
+                    out=z1[:], in0=mslice.unsqueeze(2).to_broadcast([P, 8, K]), in1=dview, op=ALU.subtract
+                )
+                z1s[hh] = z1
 
         def exp_e(hh):
             e_b = work.tile([P, HALF], F32, tag="e_b")
-            nc.scalar.activation(out=e_b[:], in_=z1s[hh][:].rearrange("p g k -> p (g k)"), func=ACT.Exp)
+            if OPT["z1"] == "v":
+                nc.scalar.activation(out=e_b[:], in_=z1s[hh][:].rearrange("p g k -> p (g k)"), func=ACT.Exp)
+            else:
+                dview = dpss[hh][:].rearrange("p t (i k) -> p (t i) k", i=2)
+                mslice = mn[:, 4 * hh : 4 * hh + 4, :].rearrange("p t i -> p (t i)")
+                for g in range(8):
+                    nc.scalar.activation(
+                        out=e_b[:, g * K : (g + 1) * K], in_=dview[:, g, :], func=ACT.Exp,
+                        bias=mslice[:, g : g + 1], scale=-1.0,
+                    )
             ebs[hh] = e_b
 
         def hi_e(hh):
@@ -235,7 +251,8 @@ def tile_image_aggregation_pa_kernel(tc, h_cluster, w2c, b2c, scores, temperatur
 
         def lo_e(hh):
             q, h = divmod(hh, 2)
-            nc.gpsimd.tensor_tensor(
+            eng = nc.gpsimd if OPT["lo"] == "g" else nc.vector
+            eng.tensor_tensor(
                 out=hl_b[:, q, 1, 4 * h : 4 * h + 4, :].rearrange("p t c -> p (t c)"),
                 in0=ebs[hh][:],
                 in1=hl_b[:, q, 0, 4 * h : 4 * h + 4, :].rearrange("p t c -> p (t c)"),
@@ -337,10 +354,7 @@ def tile_image_aggregation_pa_kernel(tc, h_cluster, w2c, b2c, scores, temperatur
         def y_half(hh):
             q, h = divmod(hh, 2)
             y_a = work.tile([P, HALF], F32, tag="y_a")
-            nc.gpsimd.tensor_scalar(
-                out=y_a[:], in0=d_a[:, q, h * HALF : (h + 1) * HALF], scalar1=-1.0,
-                scalar2=chain[q // 2]["ln_a"][:, q % 2 : q % 2 + 1], op0=ALU.mult, op1=ALU.add,
-            )
+            affine(OPT["y"], y_a[:], d_a[:, q, h * HALF : (h + 1) * HALF], chain[q // 2]["ln_a"][:, q % 2 : q % 2 + 1])
             yas[hh] = y_a
 
         def tr_y(hh):

@@ -23,7 +23,8 @@ FLOPS = 2 * B * (D * HID * N + D * K * N)
 REGROUP = ("v", "s", "v", "v", "s", "v", "s", "v")
 PLAN = {}
 ADD_ENGINE = "v"
-OPT = {"d": "s", "y": "s", "z1": "s", "lo": "g"}
+CH = 256
+OPT = {"d": "s", "y": "s", "z1": "s", "lo": "g", "hi": "v", "junk": True}
 
 
 def tile_image_aggregation_pa_kernel(tc, h_cluster, w2c, b2c, scores, temperature, out):
@@ -80,7 +81,6 @@ def tile_image_aggregation_pa_kernel(tc, h_cluster, w2c, b2c, scores, temperatur
         wc = const.tile([P, D], U32, align_bytes=64)
         ws = const.tile([P, D], U8, align_bytes=64)
         inv_t = const.tile([P, 1], F32)
-        agg = keep.tile([P, B, K], F32)
         ss = keep.tile([P, B], F32)
 
         def w_path_1():
@@ -109,10 +109,11 @@ def tile_image_aggregation_pa_kernel(tc, h_cluster, w2c, b2c, scores, temperatur
                 b, g = divmod(u, 2)
                 if g == 0:
                     grps[b] = hwork.tile([P, N, 4], BF16, tag="grp", name="grp", align_bytes=64)
-                for c in (2 * g, 2 * g + 1):
-                    dst = grps[b][:, c * 256 : (c + 1) * 256, :].rearrange("p (c i) t -> p c t i", i=4)
-                    src = raws[b][:, :, c * 256 : (c + 1) * 256].rearrange("p t (c i) -> p c t i", i=4)
-                    eng = REGROUP[(4 * b + c) % len(REGROUP)]
+                per = HALF // CH
+                for c in range(per * g, per * (g + 1)):
+                    dst = grps[b][:, c * CH : (c + 1) * CH, :].rearrange("p (c i) t -> p c t i", i=4)
+                    src = raws[b][:, :, c * CH : (c + 1) * CH].rearrange("p t (c i) -> p c t i", i=4)
+                    eng = REGROUP[(2 * per * b + c) % len(REGROUP)]
                     if eng == "v":
                         nc.vector.tensor_copy(out=dst, in_=src)
                     elif eng == "s":
@@ -188,6 +189,8 @@ def tile_image_aggregation_pa_kernel(tc, h_cluster, w2c, b2c, scores, temperatur
             nc.vector.tensor_reduce(out=m_row[:, q : q + 1], in_=s_a[:, q, :], axis=AX.X, op=ALU.max)
 
         def junk(q):
+            if not OPT["junk"]:
+                return
             jk = work.tile([P, N], BF16, tag="jk")
             nm = small.tile([P, 1], F32, tag="nm")
             nc.scalar.mul(out=nm[:], in_=m_row[:, q : q + 1], mul=-1.0)
@@ -245,9 +248,13 @@ def tile_image_aggregation_pa_kernel(tc, h_cluster, w2c, b2c, scores, temperatur
 
         def hi_e(hh):
             q, h = divmod(hh, 2)
-            nc.vector.tensor_copy(
-                out=hl_b[:, q, 0, 4 * h : 4 * h + 4, :].rearrange("p t c -> p (t c)"), in_=ebs[hh][:]
-            )
+            dst = hl_b[:, q, 0, 4 * h : 4 * h + 4, :].rearrange("p t c -> p (t c)")
+            if OPT["hi"] == "v":
+                nc.vector.tensor_copy(out=dst, in_=ebs[hh][:])
+            elif OPT["hi"] == "s":
+                nc.scalar.copy(out=dst, in_=ebs[hh][:])
+            else:
+                nc.gpsimd.tensor_scalar(out=dst, in0=ebs[hh][:], scalar1=1.0, scalar2=0.0, op0=ALU.mult, op1=ALU.add)
 
         def lo_e(hh):
             q, h = divmod(hh, 2)
@@ -286,7 +293,10 @@ def tile_image_aggregation_pa_kernel(tc, h_cluster, w2c, b2c, scores, temperatur
             nc.vector.tensor_tensor(out=am32[:], in0=ra[:], in1=mask[:], op=ALU.mult)
             am = small.tile([P, 2, 2, 2], BF16, tag="am%d" % bt)
             split(am, am32[:])
-            chain[bt] = {"am": am, "am32": am32}
+            if bt not in chain:
+                chain[bt] = {}
+            chain[bt]["am"] = am
+            chain[bt]["am32"] = am32
 
         def u_mm(bt):
             rps = ps_mv.tile([P, 2, 2, 2], F32, tag="mv", name="rps")
@@ -348,19 +358,37 @@ def tile_image_aggregation_pa_kernel(tc, h_cluster, w2c, b2c, scores, temperatur
             ln_a = small.tile([P, 2], F32, tag="ln_a%d" % bt)
             nc.scalar.activation(out=ln_a[:], in_=a_sel[:], func=ACT.Ln)
             chain[bt]["ln_a"] = ln_a
+            if OPT["y"] == "t":
+                nln_a = small.tile([P, 2], F32, tag="nln_a%d" % bt)
+                nc.scalar.mul(out=nln_a[:], in_=ln_a[:], mul=-1.0)
+                chain[bt]["nln_a"] = nln_a
 
         yas, ypss, zfs, q12, pgs = {}, {}, {}, {}, {}
 
         def y_half(hh):
             q, h = divmod(hh, 2)
+            if OPT["y"] == "t":
+                return
             y_a = work.tile([P, HALF], F32, tag="y_a")
             affine(OPT["y"], y_a[:], d_a[:, q, h * HALF : (h + 1) * HALF], chain[q // 2]["ln_a"][:, q % 2 : q % 2 + 1])
             yas[hh] = y_a
 
         def tr_y(hh):
             yps = ps_tr.tile([P, 4, P], F32, tag="tr", name="yps")
+            q, h = divmod(hh, 2)
             for t in range(4):
-                nc.tensor.transpose(yps[:, t, :], yas[hh][:, t * P : (t + 1) * P], ident_f[:])
+                if OPT["y"] == "t":
+                    nt = 4 * h + t
+                    nc.tensor.matmul(
+                        out=yps[:, t, :], lhsT=d_a[:, q, nt * P : (nt + 1) * P], rhs=ident_f[:],
+                        is_transpose=True, start=True, stop=False,
+                    )
+                    nc.tensor.matmul(
+                        out=yps[:, t, :], lhsT=chain[q // 2]["nln_a"][:, q % 2 : q % 2 + 1].to_broadcast([P, P]),
+                        rhs=ident_f[:], is_transpose=True, start=False, stop=True,
+                    )
+                else:
+                    nc.tensor.transpose(yps[:, t, :], yas[hh][:, t * P : (t + 1) * P], ident_f[:])
             ypss[hh] = yps
 
         def ln_c(bt):
@@ -374,18 +402,18 @@ def tile_image_aggregation_pa_kernel(tc, h_cluster, w2c, b2c, scores, temperatur
 
         def z_f(hh):
             bt, loc = divmod(hh, 4)
-            zf = work.tile([P, 8, K], F32, tag="zf")
-            bslice = chain[bt]["bias_f"][:, 4 * loc : 4 * loc + 4, :].rearrange("p t i -> p (t i)")
+            zf = work.tile([P, HALF], F32, tag="zf")
+            bslice = chain[bt]["bias_f"][:, 4 * loc : 4 * loc + 4, :].rearrange("p t i -> p i t")
             nc.vector.tensor_tensor(
-                out=zf[:],
-                in0=bslice.unsqueeze(2).to_broadcast([P, 8, K]),
-                in1=ypss[hh][:].rearrange("p t (i k) -> p (t i) k", i=2),
-                op=ALU.add,
+                out=zf[:].rearrange("p (i k t) -> p i k t", i=2, t=4),
+                in0=bslice.unsqueeze(2).to_broadcast([P, 2, K, 4]),
+                in1=ypss[hh][:].rearrange("p t (i k) -> p i k t", i=2),
+                op=(ALU.subtract if OPT["y"] == "t" else ALU.add),
             )
             zfs[hh] = zf
 
         def exps(hh):
-            zflat = zfs[hh][:].rearrange("p g k -> p (g k)")
+            zflat = zfs[hh][:]
             q1 = work.tile([P, HALF], F32, tag="q1")
             nc.scalar.activation(out=q1[:], in_=zflat, func=ACT.Exp)
             q2 = work.tile([P, HALF], F32, tag="q2")
@@ -394,12 +422,12 @@ def tile_image_aggregation_pa_kernel(tc, h_cluster, w2c, b2c, scores, temperatur
 
         def add_p(hh):
             q1, q2 = q12[hh]
-            pg = work.tile([P, P, 4], BF16, tag="pg", align_bytes=64)
+            pg = work.tile([P, HALF], BF16, tag="pg", align_bytes=64)
             eng = nc.gpsimd if ADD_ENGINE == "g" else nc.vector
             eng.tensor_tensor(
                 out=pg[:],
-                in0=q1[:].rearrange("p (j c) -> p c j", j=4),
-                in1=q2[:].rearrange("p (j c) -> p c j", j=4),
+                in0=q1[:],
+                in1=q2[:],
                 op=ALU.add,
             )
             pgs[hh] = pg
@@ -409,15 +437,19 @@ def tile_image_aggregation_pa_kernel(tc, h_cluster, w2c, b2c, scores, temperatur
             nc.vector.quantize_mx(
                 out=pc[:, q, g * P : (g + 1) * P].bitcast(FP8X4),
                 scales=psc[:, q, g * P : (g + 1) * P],
-                in_=pgs[hh][:].rearrange("p c j -> p (c j)"),
+                in_=pgs[hh][:],
             )
+
+        banks = {}
 
         def agg_mm(b):
             q, i = divmod(b, 2)
-            aps = ps_misc.tile([P, 2 * K], F32, tag="misc", name="aps")
+            if b % 4 == 0:
+                banks[b // 4] = ps_tr.tile([P, 4, 2 * K], F32, tag="tr", name="abank")
+            aps = banks[b // 4][:, b % 4, :]
             for g in range(2):
                 nc.tensor.matmul_mx(
-                    out=aps[:],
+                    out=aps,
                     lhsT=fc[:, b, g * D : (g + 1) * D].bitcast(FP8X4),
                     lhsT_scale=fs[:, b, g * D : (g + 1) * D],
                     rhs=pc[:, q, g * P : (g + 1) * P].bitcast(FP8X4),
@@ -425,9 +457,8 @@ def tile_image_aggregation_pa_kernel(tc, h_cluster, w2c, b2c, scores, temperatur
                     start=(g == 0),
                     stop=(g == 1),
                 )
-            nc.scalar.copy(out=agg[:, b, :], in_=aps[:, i * K : (i + 1) * K])
             sq = small.tile([P, K], F32, tag="sq")
-            nc.scalar.activation(out=sq[:], in_=agg[:, b, :], func=ACT.Square, accum_out=ss[:, b : b + 1])
+            nc.scalar.activation(out=sq[:], in_=aps[:, i * K : (i + 1) * K], func=ACT.Square, accum_out=ss[:, b : b + 1])
 
         rowmax(0)
         junk(0)
@@ -437,7 +468,18 @@ def tile_image_aggregation_pa_kernel(tc, h_cluster, w2c, b2c, scores, temperatur
         junk(1)
         tr_d(0)
         wps = w_path_1()
-        steps0 = ["v", "u", "v", "u", "v"]
+        steps0 = ["v", "u", "v", "u", "v"] if OPT["junk"] else ["u", "v", "u", "v", "u", "v"]
+        nsteps = len(steps0)
+
+        def first(bt):
+            if OPT["junk"]:
+                alpha_from(bt, r1[:, 2 * bt : 2 * bt + 2].unsqueeze(2).to_broadcast([P, 2, 2]))
+            else:
+                b0 = small.tile([P, 2 * NT, 2], F32, tag="b32%d" % bt)
+                nc.scalar.activation(out=b0[:], in_=mn[:, bt * 2 * NT : (bt + 1) * 2 * NT, :], func=ACT.Exp, scale=-1.0)
+                beta = small.tile([P, 2 * NT, 2, 2], BF16, tag="bt%d" % bt)
+                split(beta, b0[:])
+                chain[bt] = {"bt": beta}
         done = {0: 0, 1: 0}
 
         def chain_mm(bt):
@@ -449,12 +491,12 @@ def tile_image_aggregation_pa_kernel(tc, h_cluster, w2c, b2c, scores, temperatur
 
         def chain_hop(bt):
             kind = steps0[done[bt]]
-            last = done[bt] == 4
+            last = done[bt] == nsteps - 1
             if kind == "v":
                 v_hop(bt, last)
             else:
                 u_hop(bt)
-                if done[bt] == 3:
+                if done[bt] == nsteps - 2:
                     ln_alpha(bt)
             done[bt] += 1
 
@@ -478,23 +520,28 @@ def tile_image_aggregation_pa_kernel(tc, h_cluster, w2c, b2c, scores, temperatur
             if 2 <= tick < 10:
                 evac_e(tick - 2)
             if tick == 5:
-                alpha_from(0, r1[:, 0:2].unsqueeze(2).to_broadcast([P, 2, 2]))
+                first(0)
             if tick == 6:
                 chain_mm(0)
-            if tick >= 7:
+            if tick >= 7 and done[0] < nsteps - 1:
                 chain_hop(0)
                 chain_mm(0)
             if tick == 9:
-                alpha_from(1, r1[:, 2:4].unsqueeze(2).to_broadcast([P, 2, 2]))
+                first(1)
             if tick == 10:
                 chain_mm(1)
             fill("a%d" % tick)
 
+        while done[0] < nsteps - 1:
+            chain_hop(0)
+            chain_mm(0)
         for hh in range(4):
             y_half(hh)
         chain_hop(0)
         ln_c(0)
-        fill("b0")
+        while done[1] < nsteps - 5:
+            chain_hop(1)
+            chain_mm(1)
         for r in range(4):
             chain_hop(1)
             chain_mm(1)
@@ -529,6 +576,8 @@ def tile_image_aggregation_pa_kernel(tc, h_cluster, w2c, b2c, scores, temperatur
         quant_f(2 * B - 1)
         add_p(7)
         quant_p(7)
+        warm = small.tile([P, 1], F32, tag="warm")
+        nc.scalar.activation(out=warm[:], in_=q12[7][1][:, 0:1], func=ACT.Sqrt, bias=1.0, scale=0.0)
         for b in range(B):
             agg_mm(b)
         tot = ps_mv.tile([P, B], F32, tag="mv")
@@ -540,7 +589,11 @@ def tile_image_aggregation_pa_kernel(tc, h_cluster, w2c, b2c, scores, temperatur
         rn = small.tile([P, B], F32, tag="rn")
         nc.vector.reciprocal(out=rn[:], in_=nrm[:])
         res = keep.tile([P, B, K], F32)
-        nc.vector.tensor_tensor(
-            out=res[:], in0=agg[:], in1=rn[:].unsqueeze(2).to_broadcast([P, B, K]), op=ALU.mult
-        )
+        for bt in range(2):
+            nc.vector.tensor_tensor(
+                out=res[:, 4 * bt : 4 * bt + 4, :].rearrange("p (q i) k -> p q i k", i=2),
+                in0=banks[bt][:].rearrange("p (q i) (j k) -> p q (i j) k", i=2, j=2)[:, :, 0:4:3, :],
+                in1=rn[:, 4 * bt : 4 * bt + 4].rearrange("p (q i) -> p q i", i=2).unsqueeze(3).to_broadcast([P, 2, 2, K]),
+                op=ALU.mult,
+            )
         nc.sync.dma_start(out=out.rearrange("b (d k) -> d b k", k=K), in_=res[:])

@@ -20,11 +20,13 @@ HALF = N // 2
 
 FLOPS = 2 * B * (D * HID * N + D * K * N)
 
-REGROUP = ("v", "s", "v", "v", "s", "v", "s", "v")
+REGROUP = ("v", "v", "v", "v", "v", "v", "v", "v", "v", "v", "v", "v", "s", "s", "s", "v", "s", "s", "s", "v", "s", "s", "s", "v", "s", "s", "s", "v", "s", "s", "s", "v")
 PLAN = {}
-ADD_ENGINE = "v"
+ADD_ENGINE = "g"
 CH = 256
-OPT = {"d": "s", "y": "s", "z1": "s", "lo": "g", "hi": "v", "junk": True}
+QN = 1
+FN = 1
+OPT = {"d": "g", "y": "v", "z1": "s", "lo": "g", "hi": "v", "junk": True}
 
 
 def tile_image_aggregation_pa_kernel(tc, h_cluster, w2c, b2c, scores, temperature, out):
@@ -134,11 +136,14 @@ def tile_image_aggregation_pa_kernel(tc, h_cluster, w2c, b2c, scores, temperatur
                         hwork.tile([P, N], U8, tag="hs", name="hs", align_bytes=64),
                     )
                 hc, hs = hcs[b]
-                nc.vector.quantize_mx(
-                    out=hc[:, g * HALF : (g + 1) * HALF].bitcast(FP8X4),
-                    scales=hs[:, g * HALF : (g + 1) * HALF],
-                    in_=grps[b][:, g * HALF : (g + 1) * HALF, :].rearrange("p n j -> p (n j)"),
-                )
+                for z in range(QN):
+                    lo_n = g * HALF + z * (HALF // QN)
+                    hi_n = lo_n + HALF // QN
+                    nc.vector.quantize_mx(
+                        out=hc[:, lo_n:hi_n].bitcast(FP8X4),
+                        scales=hs[:, lo_n:hi_n],
+                        in_=grps[b][:, lo_n:hi_n, :].rearrange("p n j -> p (n j)"),
+                    )
                 fb = ps_f.tile([P, 4, D], F32, tag="f", name="fb")
                 fbs[u] = fb
                 for j in range(4):
@@ -161,12 +166,14 @@ def tile_image_aggregation_pa_kernel(tc, h_cluster, w2c, b2c, scores, temperatur
                 state["f"] = u + 1
                 b, g = divmod(u, 2)
                 fg = hwork.tile([P, D, 4], BF16, tag="fg", name="fg", align_bytes=64)
-                nc.vector.tensor_tensor(
-                    out=fg[:],
-                    in0=fbs[u][:].rearrange("p j d -> p d j"),
-                    in1=bias_bc[:].unsqueeze(2).to_broadcast([P, D, 4]),
-                    op=ALU.add,
-                )
+                for z in range(FN):
+                    dsl = slice(z * (D // FN), (z + 1) * (D // FN))
+                    nc.vector.tensor_tensor(
+                        out=fg[:, dsl, :],
+                        in0=fbs[u][:, :, dsl].rearrange("p j d -> p d j"),
+                        in1=bias_bc[:, dsl].unsqueeze(2).to_broadcast([P, D // FN, 4]),
+                        op=ALU.add,
+                    )
                 fgs[u] = fg
                 if u >= 1:
                     quant_f(u - 1)

@@ -20,13 +20,13 @@ HALF = N // 2
 
 FLOPS = 2 * B * (D * HID * N + D * K * N)
 
-REGROUP = ("v", "v", "v", "v", "v", "v", "v", "v", "v", "v", "v", "v", "s", "s", "s", "v", "s", "s", "s", "v", "s", "s", "s", "v", "s", "s", "s", "v", "s", "s", "s", "v")
+REGROUP = ("v", "v", "v", "v", "v", "v", "v", "v", "s", "s", "s", "s", "s", "s", "s", "v", "s", "s", "s", "s", "s", "s", "s", "v", "s", "s", "s", "s", "s", "s", "s", "v")
 PLAN = {}
-ADD_ENGINE = "g"
+ADD_ENGINE = "v"
 CH = 256
 QN = 1
 FN = 1
-OPT = {"d": "g", "y": "v", "z1": "s", "lo": "g", "hi": "v", "junk": True}
+OPT = {"d": "v", "y": "v", "z1": "s", "lo": "v", "hi": "v", "junk": True}
 
 
 def tile_image_aggregation_pa_kernel(tc, h_cluster, w2c, b2c, scores, temperature, out):

@@ -20,13 +20,13 @@ HALF = N // 2
 
 FLOPS = 2 * B * (D * HID * N + D * K * N)
 
-REGROUP = ("v", "v", "v", "v", "v", "v", "v", "v", "s", "s", "s", "s", "s", "s", "s", "v", "s", "s", "s", "s", "s", "s", "s", "v", "s", "s", "s", "s", "s", "s", "s", "v")
+REGROUP = ("v", "v", "v", "v", "s", "s", "s", "s", "s", "s", "s", "s", "s", "s", "s", "s", "s", "s", "s", "s", "s", "s", "s", "s", "s", "s", "s", "s", "s", "s", "s", "s")
 PLAN = {}
 ADD_ENGINE = "v"
 CH = 256
 QN = 1
 FN = 1
-OPT = {"d": "v", "y": "v", "z1": "s", "lo": "v", "hi": "v", "junk": True}
+OPT = {"d": "v", "y": "v", "z1": "s", "lo": "v", "hi": "v", "junk": False}
 
 
 def tile_image_aggregation_pa_kernel(tc, h_cluster, w2c, b2c, scores, temperature, out):

@@ -20,13 +20,13 @@ HALF = N // 2
 
 FLOPS = 2 * B * (D * HID * N + D * K * N)
 
-REGROUP = ("v", "v", "v", "v", "s", "s", "s", "s", "s", "s", "s", "s", "s", "s", "s", "s", "s", "s", "s", "s", "s", "s", "s", "s", "s", "s", "s", "s", "s", "s", "s", "s")
+REGROUP = ("v", "v", "v", "v", "v", "v", "v", "v", "s", "s", "s", "v", "s", "s", "s", "v", "s", "s", "s", "v", "s", "s", "s", "v", "s", "s", "s", "v", "s", "s", "s", "v")
 PLAN = {}
 ADD_ENGINE = "v"
 CH = 256
 QN = 1
 FN = 1
-OPT = {"d": "v", "y": "v", "z1": "s", "lo": "v", "hi": "v", "junk": False}
+OPT = {"d": "v", "y": "v", "z1": "s", "lo": "v", "hi": "v", "junk": True}
 
 
 def tile_image_aggregation_pa_kernel(tc, h_cluster, w2c, b2c, scores, temperature, out):

@@ -20,7 +20,7 @@ HALF = N // 2
 
 FLOPS = 2 * B * (D * HID * N + D * K * N)
 
-REGROUP = ("v", "v", "v", "v", "v", "v", "v", "v", "s", "s", "s", "v", "s", "s", "s", "v", "s", "s", "s", "v", "s", "s", "s", "v", "s", "s", "s", "v", "s", "s", "s", "v")
+REGROUP = ("v", "v", "v", "v", "v", "v", "v", "v", "s", "s", "v", "s", "s", "v", "s", "s", "v", "s", "s", "v", "s", "s", "v", "s", "s", "v", "s", "s", "v", "s", "s", "v")
 PLAN = {}
 ADD_ENGINE = "v"
 CH = 256

from contextlib import ExitStack

import concourse.mybir as mybir
from concourse.masks import make_identity

F32 = mybir.dt.float32
BF16 = mybir.dt.bfloat16
U32 = mybir.dt.uint32
U8 = mybir.dt.uint8
FP8X4 = mybir.dt.float8_e4m3fn_x4
ALU = mybir.AluOpType
ACT = mybir.ActivationFunctionType
AX = mybir.AxisListType

P = 128
B, HID, N, D, K = 8, 512, 1024, 128, 64
Q = B // 2
NT = N // P
HALF = N // 2

FLOPS = 2 * B * (D * HID * N + D * K * N)

REGROUP = ("v", "v", "v", "v", "v", "v", "v", "v", "s", "s", "v", "s", "s", "v", "s", "s", "v", "s", "s", "v", "s", "s", "v", "s", "s", "v", "s", "s", "v", "s", "s", "v")
PLAN = {}
ADD_ENGINE = "v"
CH = 256
QN = 1
FN = 1
OPT = {"d": "v", "y": "v", "z1": "s", "lo": "v", "hi": "v", "junk": True}


def tile_image_aggregation_pa_kernel(tc, h_cluster, w2c, b2c, scores, temperature, out):
    nc = tc.nc
    with ExitStack() as ctx:
        const = ctx.enter_context(tc.tile_pool(name="const", bufs=1))
        keep = ctx.enter_context(tc.tile_pool(name="keep", bufs=1))
        work = ctx.enter_context(tc.tile_pool(name="work", bufs=3))
        small = ctx.enter_context(tc.tile_pool(name="small", bufs=2))
        hraw = ctx.enter_context(tc.tile_pool(name="hraw", bufs=6))
        hwork = ctx.enter_context(tc.tile_pool(name="hwork", bufs=3))
        ps_tr = ctx.enter_context(tc.psum_pool(name="ps_tr", bufs=3))
        ps_f = ctx.enter_context(tc.psum_pool(name="ps_f", bufs=2))
        ps_mv = ctx.enter_context(tc.psum_pool(name="ps_mv", bufs=2))
        ps_misc = ctx.enter_context(tc.psum_pool(name="ps_misc", bufs=1))

        s_a = keep.tile([P, Q, N], BF16)
        s_view = scores.rearrange("(q i) k n -> (i k) q n", i=2)
        for q in range(Q):
            nc.sync.dma_start(out=s_a[:, q, :], in_=s_view[:, q, :])
        bias_bc = const.tile([P, D], BF16)
        nc.scalar.dma_start(out=bias_bc[:], in_=b2c.partition_broadcast(P))
        temp = const.tile([P, 1], BF16)
        nc.scalar.dma_start(out=temp[:], in_=temperature.partition_broadcast(P))
        w_sb = const.tile([P, HID], BF16)
        nc.sync.dma_start(out=w_sb[:], in_=w2c)
        raws = []
        for b in range(B):
            raw = hraw.tile([P, 4, N], BF16, tag="raw")
            nc.sync.dma_start(out=raw[:], in_=h_cluster[b].rearrange("(p j) n -> p j n", j=4))
            raws.append(raw)

        ident_f = const.tile([P, P], F32)
        make_identity(nc, ident_f[:])
        ident_b = const.tile([P, P], BF16)
        make_identity(nc, ident_b[:])
        ones_f = const.tile([P, P], F32)
        nc.vector.memset(ones_f[:], 1.0)
        mask = const.tile([P, 2, 2], F32)
        nc.vector.memset(mask[:], 0.0)
        nc.vector.memset(mask[0:64, :, 0:1], 1.0)
        nc.vector.memset(mask[64:128, :, 1:2], 1.0)

        m_row = keep.tile([P, Q], F32)
        r1 = keep.tile([P, Q], F32)
        d_a = keep.tile([P, Q, N], F32)
        mn = keep.tile([P, Q * NT, 2], F32)
        hl_b = keep.tile([P, Q, 2, NT, P], BF16)
        hl_a = keep.tile([P, Q, 2, N], BF16)
        pc = keep.tile([P, Q, 2 * P], U32, align_bytes=64)
        psc = keep.tile([P, Q, 2 * P], U8, align_bytes=64)
        fc = keep.tile([P, B, 2 * D], U32, align_bytes=64)
        fs = keep.tile([P, B, 2 * D], U8, align_bytes=64)
        wc = const.tile([P, D], U32, align_bytes=64)
        ws = const.tile([P, D], U8, align_bytes=64)
        inv_t = const.tile([P, 1], F32)
        ss = keep.tile([P, B], F32)

        def w_path_1():
            w_perm = const.tile([P, 4, P], BF16)
            nc.vector.tensor_copy(out=w_perm[:], in_=w_sb[:].rearrange("d (p j) -> d j p", j=4))
            wps = ps_misc.tile([P, 4, D], BF16, tag="misc")
            for j in range(4):
                nc.tensor.transpose(wps[:, j, :], w_perm[:, j, :], ident_b[:])
            return wps

        def w_path_2(wps):
            wg = const.tile([P, D, 4], BF16, align_bytes=64)
            nc.vector.tensor_copy(out=wg[:], in_=wps[:].rearrange("p j d -> p d j"))
            nc.vector.reciprocal(out=inv_t[:], in_=temp[:])
            nc.vector.quantize_mx(out=wc[:].bitcast(FP8X4), scales=ws[:], in_=wg[:].rearrange("p d j -> p (d j)"))

        state = {"r": 0, "q": 0, "f": 0}
        grps, hcs, fbs, fgs = {}, {}, {}, {}

        def fill_r(count):
            for x in range(count):
                u = state["r"]
                if u >= 2 * B:
                    return
                state["r"] = u + 1
                b, g = divmod(u, 2)
                if g == 0:
                    grps[b] = hwork.tile([P, N, 4], BF16, tag="grp", name="grp", align_bytes=64)
                per = HALF // CH
                for c in range(per * g, per * (g + 1)):
                    dst = grps[b][:, c * CH : (c + 1) * CH, :].rearrange("p (c i) t -> p c t i", i=4)
                    src = raws[b][:, :, c * CH : (c + 1) * CH].rearrange("p t (c i) -> p c t i", i=4)
                    eng = REGROUP[(2 * per * b + c) % len(REGROUP)]
                    if eng == "v":
                        nc.vector.tensor_copy(out=dst, in_=src)
                    elif eng == "s":
                        nc.scalar.copy(out=dst, in_=src)
                    else:
                        nc.gpsimd.tensor_scalar(out=dst, in0=src, scalar1=1.0, scalar2=0.0, op0=ALU.mult, op1=ALU.add)

        def fill_q(count):
            for x in range(count):
                u = state["q"]
                if u >= 2 * B or u >= state["r"]:
                    return
                state["q"] = u + 1
                b, g = divmod(u, 2)
                if g == 0:
                    hcs[b] = (
                        hwork.tile([P, N], U32, tag="hc", name="hc", align_bytes=64),
                        hwork.tile([P, N], U8, tag="hs", name="hs", align_bytes=64),
                    )
                hc, hs = hcs[b]
                for z in range(QN):
                    lo_n = g * HALF + z * (HALF // QN)
                    hi_n = lo_n + HALF // QN
                    nc.vector.quantize_mx(
                        out=hc[:, lo_n:hi_n].bitcast(FP8X4),
                        scales=hs[:, lo_n:hi_n],
                        in_=grps[b][:, lo_n:hi_n, :].rearrange("p n j -> p (n j)"),
                    )
                fb = ps_f.tile([P, 4, D], F32, tag="f", name="fb")
                fbs[u] = fb
                for j in range(4):
                    nt = 4 * g + j
                    nc.tensor.matmul_mx(
                        out=fb[:, j, :],
                        lhsT=hc[:, nt * P : (nt + 1) * P].bitcast(FP8X4),
                        lhsT_scale=hs[:, nt * P : (nt + 1) * P],
                        rhs=wc[:].bitcast(FP8X4),
                        rhs_scale=ws[:],
                        start=True,
                        stop=True,
                    )

        def fill_f(count):
            for x in range(count):
                u = state["f"]
                if u >= 2 * B or u >= state["q"]:
                    return
                state["f"] = u + 1
                b, g = divmod(u, 2)
                fg = hwork.tile([P, D, 4], BF16, tag="fg", name="fg", align_bytes=64)
                for z in range(FN):
                    dsl = slice(z * (D // FN), (z + 1) * (D // FN))
                    nc.vector.tensor_tensor(
                        out=fg[:, dsl, :],
                        in0=fbs[u][:, :, dsl].rearrange("p j d -> p d j"),
                        in1=bias_bc[:, dsl].unsqueeze(2).to_broadcast([P, D // FN, 4]),
                        op=ALU.add,
                    )
                fgs[u] = fg
                if u >= 1:
                    quant_f(u - 1)

        def quant_f(u):
            b, g = divmod(u, 2)
            nc.vector.quantize_mx(
                out=fc[:, b, g * D : (g + 1) * D].bitcast(FP8X4),
                scales=fs[:, b, g * D : (g + 1) * D],
                in_=fgs[u][:].rearrange("p d j -> p (d j)"),
            )

        def fill(key):
            r, qq, f = PLAN.get(key, (0, 0, 0))
            fill_f(f)
            fill_q(qq)
            fill_r(r)

        def rowmax(q):
            nc.vector.tensor_reduce(out=m_row[:, q : q + 1], in_=s_a[:, q, :], axis=AX.X, op=ALU.max)

        def junk(q):
            if not OPT["junk"]:
                return
            jk = work.tile([P, N], BF16, tag="jk")
            nm = small.tile([P, 1], F32, tag="nm")
            nc.scalar.mul(out=nm[:], in_=m_row[:, q : q + 1], mul=-1.0)
            nc.scalar.activation(
                out=jk[:], in_=s_a[:, q, :], func=ACT.Exp, bias=nm[:, 0:1], accum_out=r1[:, q : q + 1]
            )

        def affine(eng, dst, src, col):
            if eng == "s":
                nc.scalar.activation(out=dst, in_=src, func=ACT.Identity, bias=col, scale=-1.0)
            elif eng == "v":
                nc.vector.tensor_scalar(out=dst, in0=src, scalar1=-1.0, scalar2=col, op0=ALU.mult, op1=ALU.add)
            else:
                nc.gpsimd.tensor_scalar(out=dst, in0=src, scalar1=-1.0, scalar2=col, op0=ALU.mult, op1=ALU.add)

        def d_half(hh):
            q, h = divmod(hh, 2)
            sl = slice(h * HALF, (h + 1) * HALF)
            affine(OPT["d"], d_a[:, q, sl], s_a[:, q, sl], m_row[:, q : q + 1])

        dpss, z1s, ebs, tpss = {}, {}, {}, {}

        def tr_d(hh):
            q, h = divmod(hh, 2)
            dps = ps_tr.tile([P, 4, P], F32, tag="tr", name="dps")
            for t in range(4):
                nt = 4 * h + t
                nc.tensor.transpose(dps[:, t, :], d_a[:, q, nt * P : (nt + 1) * P], ident_f[:])
            dpss[hh] = dps

        def min_z(hh):
            dview = dpss[hh][:].rearrange("p t (i k) -> p (t i) k", i=2)
            mslice = mn[:, 4 * hh : 4 * hh + 4, :].rearrange("p t i -> p (t i)")
            nc.vector.tensor_reduce(out=mslice, in_=dview, axis=AX.X, op=ALU.min)
            if OPT["z1"] == "v":
                z1 = work.tile([P, 8, K], F32, tag="z1")
                nc.vector.tensor_tensor(
                    out=z1[:], in0=mslice.unsqueeze(2).to_broadcast([P, 8, K]), in1=dview, op=ALU.subtract
                )
                z1s[hh] = z1

        def exp_e(hh):
            e_b = work.tile([P, HALF], F32, tag="e_b")
            if OPT["z1"] == "v":
                nc.scalar.activation(out=e_b[:], in_=z1s[hh][:].rearrange("p g k -> p (g k)"), func=ACT.Exp)
            else:
                dview = dpss[hh][:].rearrange("p t (i k) -> p (t i) k", i=2)
                mslice = mn[:, 4 * hh : 4 * hh + 4, :].rearrange("p t i -> p (t i)")
                for g in range(8):
                    nc.scalar.activation(
                        out=e_b[:, g * K : (g + 1) * K], in_=dview[:, g, :], func=ACT.Exp,
                        bias=mslice[:, g : g + 1], scale=-1.0,
                    )
            ebs[hh] = e_b

        def hi_e(hh):
            q, h = divmod(hh, 2)
            dst = hl_b[:, q, 0, 4 * h : 4 * h + 4, :].rearrange("p t c -> p (t c)")
            if OPT["hi"] == "v":
                nc.vector.tensor_copy(out=dst, in_=ebs[hh][:])
            elif OPT["hi"] == "s":
                nc.scalar.copy(out=dst, in_=ebs[hh][:])
            else:
                nc.gpsimd.tensor_scalar(out=dst, in0=ebs[hh][:], scalar1=1.0, scalar2=0.0, op0=ALU.mult, op1=ALU.add)

        def lo_e(hh):
            q, h = divmod(hh, 2)
            eng = nc.gpsimd if OPT["lo"] == "g" else nc.vector
            eng.tensor_tensor(
                out=hl_b[:, q, 1, 4 * h : 4 * h + 4, :].rearrange("p t c -> p (t c)"),
                in0=ebs[hh][:],
                in1=hl_b[:, q, 0, 4 * h : 4 * h + 4, :].rearrange("p t c -> p (t c)"),
                op=ALU.subtract,
            )

        def tr_e(hh):
            q, h = divmod(hh, 2)
            tps = ps_tr.tile([P, 2, 4, P], BF16, tag="tr", name="tps")
            for s in range(2):
                for t in range(4):
                    nc.tensor.transpose(tps[:, s, t, :], hl_b[:, q, s, 4 * h + t, :], ident_b[:])
            tpss[hh] = tps

        def evac_e(hh):
            q, h = divmod(hh, 2)
            nc.scalar.copy(
                out=hl_a[:, q, :, h * HALF : (h + 1) * HALF], in_=tpss[hh][:].rearrange("p s t n -> p s (t n)")
            )

        def split(dst, src):
            nc.vector.tensor_copy(out=dst[:, :, 0, :], in_=src)
            nc.vector.tensor_tensor(out=dst[:, :, 1, :], in0=src, in1=dst[:, :, 0, :], op=ALU.subtract)

        chain = {}

        def alpha_from(bt, rsum):
            ra = small.tile([P, 2, 2], F32, tag="ra%d" % bt)
            nc.vector.reciprocal(out=ra[:], in_=rsum)
            am32 = small.tile([P, 2, 2], F32, tag="am32%d" % bt)
            nc.vector.tensor_tensor(out=am32[:], in0=ra[:], in1=mask[:], op=ALU.mult)
            am = small.tile([P, 2, 2, 2], BF16, tag="am%d" % bt)
            split(am, am32[:])
            if bt not in chain:
                chain[bt] = {}
            chain[bt]["am"] = am
            chain[bt]["am32"] = am32

        def u_mm(bt):
            rps = ps_mv.tile([P, 2, 2, 2], F32, tag="mv", name="rps")
            beta = chain[bt]["bt"]
            for ql in range(2):
                q = 2 * bt + ql
                step = 0
                for nt in range(NT):
                    for s in range(2):
                        nc.tensor.matmul(
                            out=rps[:, ql].rearrange("p s i -> p (s i)"),
                            lhsT=hl_b[:, q, s, nt, :],
                            rhs=beta[:, ql * NT + nt].rearrange("p s i -> p (s i)"),
                            start=(step == 0),
                            stop=(step == 2 * NT - 1),
                        )
                        step += 1
            chain[bt]["rps"] = rps

        def u_hop(bt):
            rs = small.tile([P, 2, 2], F32, tag="rs%d" % bt)
            nc.vector.tensor_reduce(
                out=rs[:], in_=chain[bt]["rps"][:].rearrange("p q s i -> p q i s"), axis=AX.X, op=ALU.add
            )
            alpha_from(bt, rs[:])

        def v_mm(bt):
            cps = ps_mv.tile([P, 2 * NT, 2, 2], F32, tag="mv", name="cps")
            am = chain[bt]["am"]
            for ql in range(2):
                q = 2 * bt + ql
                for nt in range(NT):
                    for s in range(2):
                        nc.tensor.matmul(
                            out=cps[:, ql * NT + nt].rearrange("p s i -> p (s i)"),
                            lhsT=hl_a[:, q, s, nt * P : (nt + 1) * P],
                            rhs=am[:, ql].rearrange("p s i -> p (s i)"),
                            start=(s == 0),
                            stop=(s == 1),
                        )
            chain[bt]["cps"] = cps

        def v_hop(bt, last):
            cs = small.tile([P, 2 * NT, 2], F32, tag="cs%d" % bt)
            nc.vector.tensor_reduce(
                out=cs[:], in_=chain[bt]["cps"][:].rearrange("p g s i -> p g i s"), axis=AX.X, op=ALU.add
            )
            chain[bt]["cs"] = cs
            if not last:
                b32 = small.tile([P, 2 * NT, 2], F32, tag="b32%d" % bt)
                nc.vector.reciprocal(out=b32[:], in_=cs[:])
                beta = small.tile([P, 2 * NT, 2, 2], BF16, tag="bt%d" % bt)
                split(beta, b32[:])
                chain[bt]["bt"] = beta

        def ln_alpha(bt):
            a_sel = small.tile([P, 2], F32, tag="a_sel%d" % bt)
            nc.vector.tensor_reduce(out=a_sel[:], in_=chain[bt]["am32"][:], axis=AX.X, op=ALU.add)
            ln_a = small.tile([P, 2], F32, tag="ln_a%d" % bt)
            nc.scalar.activation(out=ln_a[:], in_=a_sel[:], func=ACT.Ln)
            chain[bt]["ln_a"] = ln_a
            if OPT["y"] == "t":
                nln_a = small.tile([P, 2], F32, tag="nln_a%d" % bt)
                nc.scalar.mul(out=nln_a[:], in_=ln_a[:], mul=-1.0)
                chain[bt]["nln_a"] = nln_a

        yas, ypss, zfs, q12, pgs = {}, {}, {}, {}, {}

        def y_half(hh):
            q, h = divmod(hh, 2)
            if OPT["y"] == "t":
                return
            y_a = work.tile([P, HALF], F32, tag="y_a")
            affine(OPT["y"], y_a[:], d_a[:, q, h * HALF : (h + 1) * HALF], chain[q // 2]["ln_a"][:, q % 2 : q % 2 + 1])
            yas[hh] = y_a

        def tr_y(hh):
            yps = ps_tr.tile([P, 4, P], F32, tag="tr", name="yps")
            q, h = divmod(hh, 2)
            for t in range(4):
                if OPT["y"] == "t":
                    nt = 4 * h + t
                    nc.tensor.matmul(
                        out=yps[:, t, :], lhsT=d_a[:, q, nt * P : (nt + 1) * P], rhs=ident_f[:],
                        is_transpose=True, start=True, stop=False,
                    )
                    nc.tensor.matmul(
                        out=yps[:, t, :], lhsT=chain[q // 2]["nln_a"][:, q % 2 : q % 2 + 1].to_broadcast([P, P]),
                        rhs=ident_f[:], is_transpose=True, start=False, stop=True,
                    )
                else:
                    nc.tensor.transpose(yps[:, t, :], yas[hh][:, t * P : (t + 1) * P], ident_f[:])
            ypss[hh] = yps

        def ln_c(bt):
            lc = small.tile([P, 2 * NT, 2], F32, tag="lc%d" % bt)
            nc.scalar.activation(out=lc[:], in_=chain[bt]["cs"][:], func=ACT.Ln)
            bias_f = small.tile([P, 2 * NT, 2], F32, tag="bias_f%d" % bt)
            nc.vector.tensor_tensor(
                out=bias_f[:], in0=mn[:, bt * 2 * NT : (bt + 1) * 2 * NT, :], in1=lc[:], op=ALU.subtract
            )
            chain[bt]["bias_f"] = bias_f

        def z_f(hh):
            bt, loc = divmod(hh, 4)
            zf = work.tile([P, HALF], F32, tag="zf")
            bslice = chain[bt]["bias_f"][:, 4 * loc : 4 * loc + 4, :].rearrange("p t i -> p i t")
            nc.vector.tensor_tensor(
                out=zf[:].rearrange("p (i k t) -> p i k t", i=2, t=4),
                in0=bslice.unsqueeze(2).to_broadcast([P, 2, K, 4]),
                in1=ypss[hh][:].rearrange("p t (i k) -> p i k t", i=2),
                op=(ALU.subtract if OPT["y"] == "t" else ALU.add),
            )
            zfs[hh] = zf

        def exps(hh):
            zflat = zfs[hh][:]
            q1 = work.tile([P, HALF], F32, tag="q1")
            nc.scalar.activation(out=q1[:], in_=zflat, func=ACT.Exp)
            q2 = work.tile([P, HALF], F32, tag="q2")
            nc.scalar.activation(out=q2[:], in_=zflat, func=ACT.Exp, scale=inv_t[:, 0:1])
            q12[hh] = (q1, q2)

        def add_p(hh):
            q1, q2 = q12[hh]
            pg = work.tile([P, HALF], BF16, tag="pg", align_bytes=64)
            eng = nc.gpsimd if ADD_ENGINE == "g" else nc.vector
            eng.tensor_tensor(
                out=pg[:],
                in0=q1[:],
                in1=q2[:],
                op=ALU.add,
            )
            pgs[hh] = pg

        def quant_p(hh):
            q, g = divmod(hh, 2)
            nc.vector.quantize_mx(
                out=pc[:, q, g * P : (g + 1) * P].bitcast(FP8X4),
                scales=psc[:, q, g * P : (g + 1) * P],
                in_=pgs[hh][:],
            )

        banks = {}

        def agg_mm(b):
            q, i = divmod(b, 2)
            if b % 4 == 0:
                banks[b // 4] = ps_tr.tile([P, 4, 2 * K], F32, tag="tr", name="abank")
            aps = banks[b // 4][:, b % 4, :]
            for g in range(2):
                nc.tensor.matmul_mx(
                    out=aps,
                    lhsT=fc[:, b, g * D : (g + 1) * D].bitcast(FP8X4),
                    lhsT_scale=fs[:, b, g * D : (g + 1) * D],
                    rhs=pc[:, q, g * P : (g + 1) * P].bitcast(FP8X4),
                    rhs_scale=psc[:, q, g * P : (g + 1) * P],
                    start=(g == 0),
                    stop=(g == 1),
                )
            sq = small.tile([P, K], F32, tag="sq")
            nc.scalar.activation(out=sq[:], in_=aps[:, i * K : (i + 1) * K], func=ACT.Square, accum_out=ss[:, b : b + 1])

        rowmax(0)
        junk(0)
        d_half(0)
        d_half(1)
        rowmax(1)
        junk(1)
        tr_d(0)
        wps = w_path_1()
        steps0 = ["v", "u", "v", "u", "v"] if OPT["junk"] else ["u", "v", "u", "v", "u", "v"]
        nsteps = len(steps0)

        def first(bt):
            if OPT["junk"]:
                alpha_from(bt, r1[:, 2 * bt : 2 * bt + 2].unsqueeze(2).to_broadcast([P, 2, 2]))
            else:
                b0 = small.tile([P, 2 * NT, 2], F32, tag="b32%d" % bt)
                nc.scalar.activation(out=b0[:], in_=mn[:, bt * 2 * NT : (bt + 1) * 2 * NT, :], func=ACT.Exp, scale=-1.0)
                beta = small.tile([P, 2 * NT, 2, 2], BF16, tag="bt%d" % bt)
                split(beta, b0[:])
                chain[bt] = {"bt": beta}
        done = {0: 0, 1: 0}

        def chain_mm(bt):
            kind = steps0[done[bt]]
            if kind == "v":
                v_mm(bt)
            else:
                u_mm(bt)

        def chain_hop(bt):
            kind = steps0[done[bt]]
            last = done[bt] == nsteps - 1
            if kind == "v":
                v_hop(bt, last)
            else:
                u_hop(bt)
                if done[bt] == nsteps - 2:
                    ln_alpha(bt)
            done[bt] += 1

        for tick in range(11):
            if tick < 8:
                min_z(tick)
                exp_e(tick)
            if tick + 2 < 8:
                d_half(tick + 2)
            if tick + 1 < 8:
                tr_d(tick + 1)
            if tick in (1, 3):
                rowmax(tick // 2 + 2)
                junk(tick // 2 + 2)
            if 1 <= tick < 9:
                hi_e(tick - 1)
                lo_e(tick - 1)
                tr_e(tick - 1)
            if tick == 2:
                w_path_2(wps)
            if 2 <= tick < 10:
                evac_e(tick - 2)
            if tick == 5:
                first(0)
            if tick == 6:
                chain_mm(0)
            if tick >= 7 and done[0] < nsteps - 1:
                chain_hop(0)
                chain_mm(0)
            if tick == 9:
                first(1)
            if tick == 10:
                chain_mm(1)
            fill("a%d" % tick)

        while done[0] < nsteps - 1:
            chain_hop(0)
            chain_mm(0)
        for hh in range(4):
            y_half(hh)
        chain_hop(0)
        ln_c(0)
        while done[1] < nsteps - 5:
            chain_hop(1)
            chain_mm(1)
        for r in range(4):
            chain_hop(1)
            chain_mm(1)
            fill("c%d" % r)
            tr_y(r)
            z_f(r)
            exps(r)
            fill("d%d" % r)
            add_p(r)
            fill("e%d" % r)
            quant_p(r)
            if r % 2 == 1:
                fill("f%d" % r)
        for hh in range(4, 8):
            y_half(hh)
        fill("g")
        chain_hop(1)
        ln_c(1)
        for r in range(4, 8):
            tr_y(r)
            z_f(r)
            exps(r)
            fill("h%d" % r)
            if r > 4:
                add_p(r - 1)
                quant_p(r - 1)
        fill_r(99)
        fill_q(99)
        fill_f(99)
        fill_q(99)
        fill_f(99)
        quant_f(2 * B - 1)
        add_p(7)
        quant_p(7)
        warm = small.tile([P, 1], F32, tag="warm")
        nc.scalar.activation(out=warm[:], in_=q12[7][1][:, 0:1], func=ACT.Sqrt, bias=1.0, scale=0.0)
        for b in range(B):
            agg_mm(b)
        tot = ps_mv.tile([P, B], F32, tag="mv")
        nc.tensor.matmul(out=tot[:], lhsT=ones_f[:], rhs=ss[:], start=True, stop=True)
        tmax = small.tile([P, B], F32, tag="tmax")
        nc.vector.tensor_scalar_max(out=tmax[:], in0=tot[:], scalar1=1e-24)
        nrm = small.tile([P, B], F32, tag="nrm")
        nc.scalar.activation(out=nrm[:], in_=tmax[:], func=ACT.Sqrt)
        rn = small.tile([P, B], F32, tag="rn")
        nc.vector.reciprocal(out=rn[:], in_=nrm[:])
        res = keep.tile([P, B, K], F32)
        for bt in range(2):
            nc.vector.tensor_tensor(
                out=res[:, 4 * bt : 4 * bt + 4, :].rearrange("p (q i) k -> p q i k", i=2),
                in0=banks[bt][:].rearrange("p (q i) (j k) -> p q (i j) k", i=2, j=2)[:, :, 0:4:3, :],
                in1=rn[:, 4 * bt : 4 * bt + 4].rearrange("p (q i) -> p q i", i=2).unsqueeze(3).to_broadcast([P, 2, 2, K]),
                op=ALU.mult,
            )
        nc.sync.dma_start(out=out.rearrange("b (d k) -> d b k", k=K), in_=res[:])
